import numpy as np
import ml_dtypes


def mxq(x, axis, fmt="e4m3"):
    dtype, down = {"e4m3": (ml_dtypes.float8_e4m3fn, 7), "e5m2": (ml_dtypes.float8_e5m2, 14)}[fmt]
    v = np.moveaxis(np.asarray(x, np.float32).astype(ml_dtypes.bfloat16).astype(np.float64), axis, -1)
    blocks = v.reshape(v.shape[:-1] + (-1, 32))
    amax = np.abs(blocks).max(-1, keepdims=True)
    byte = np.maximum(np.where(amax > 0, np.frexp(amax)[1] - 1 + 127, 0) - down, 1)
    scale = np.exp2(byte - 127.0)
    codes = (blocks / scale).astype(np.float32).astype(dtype).astype(np.float64)
    return np.moveaxis((codes * scale).reshape(v.shape), -1, axis)


WIDE = False


def mx_kscale(k):
    if not WIDE:
        return np.ones(k)
    levels = np.array([10, -10, 5, -5, 0])
    a = np.random.permutation(np.resize(levels, k // 512 * 4)).reshape(k // 512, 4)
    idx = np.arange(k)
    return np.exp2(a[idx // 512, idx % 128 // 32])


BF16 = ml_dtypes.bfloat16


def bf(x):
    return np.asarray(x, np.float32).astype(BF16)


def f64(x):
    return np.asarray(x).astype(np.float64)


B, IN, HID, N, NM = 2, 128, 384, 512, 5
C = IN + HID


def setup_inputs():
    s = mx_kscale(N)
    return {"x": bf(np.random.standard_normal((B, C, N)) * s),
            "support0": bf(np.random.standard_normal((N, N)) * 0.7 / np.sqrt(N) * s[:, None] / s[None, :]),
            "support1": bf(np.random.standard_normal((N, N)) * 0.7 / np.sqrt(N) * s[:, None] / s[None, :])}


def reference(x, support0, support1):
    x0 = f64(x)
    xq = mxq(x0, 2, "e4m3")
    a0q = mxq(f64(support0).T, 0, "e4m3")
    a1q = mxq(f64(support1).T, 0, "e4m3")
    x1_0 = xq @ a0q
    x2_0 = 2.0 * (mxq(x1_0, 2, "e4m3") @ a0q) - x0
    x1_1 = xq @ a1q
    x2_1 = 2.0 * (mxq(x1_1, 2, "e4m3") @ a1q) - x0
    return np.concatenate([x1_0, x2_0, x1_1, x2_1], axis=1)

@@ -1,0 +1,216 @@
+from contextlib import ExitStack
+
+import concourse.mybir as mybir
+from concourse.masks import make_identity
+
+F32 = mybir.dt.float32
+BF16 = mybir.dt.bfloat16
+U32 = mybir.dt.uint32
+U8 = mybir.dt.uint8
+FP8X4 = mybir.dt.float8_e4m3fn_x4
+MULT = mybir.AluOpType.mult
+SUB = mybir.AluOpType.subtract
+P = 128
+FLOPS = 4 * 2 * 1024 * 512 * 512
+MANUAL = True
+
+ORDER = (
+    ("L", "a00", "SP"), ("L", "a01", "SP"), ("L", "x0", "SP"), ("L", "x1", "SP"), ("L", "xb1", "SP"),
+    ("L", "a1", "SP"), ("T", "a00", "PE"), ("T", "a01", "PE"), ("E", "a00", "V"), ("T", "x0", "PE"),
+    ("E", "a01", "S"), ("Q", "a00", "V"), ("T", "x1", "PE"), ("E", "x0", "S"), ("Q", "a01", "V"),
+    ("E", "x1", "S"), ("Q", "x0", "V"), ("Q", "x1", "V"), ("S1", "00", "PE"), ("S1", "01", "PE"),
+    ("a", "00", "S"), ("T", "x2", "PE"), ("a", "01", "S"), ("st", "a001", "SP"), ("S1", "02", "PE"),
+    ("E", "x2", "V"), ("S1", "03", "PE"), ("a", "02", "S"), ("st", "a011", "SP"), ("T", "x3", "PE"),
+    ("Q", "x2", "V"), ("a", "03", "S"), ("T", "a10", "PE"), ("E", "x3", "V"), ("st", "a022", "SP"),
+    ("S1", "04", "PE"), ("Q", "x3", "V"), ("S1", "05", "PE"), ("a", "04", "S"), ("E", "a10", "V"),
+    ("T", "a11", "PE"), ("a", "05", "S"), ("Q", "a10", "V"), ("S1", "06", "PE"), ("E", "a11", "V"),
+    ("S1", "07", "PE"), ("a", "06", "S"), ("st", "a042", "SP"), ("1T", "00", "PE"), ("Q", "a11", "V"),
+    ("1T", "01", "PE"), ("a", "07", "S"), ("c", "00", "V"), ("S1", "10", "PE"), ("c", "01", "V"),
+    ("st", "a062", "SP"), ("S1", "11", "PE"), ("a", "10", "S"), ("1T", "02", "PE"), ("Q", "y00", "V"),
+    ("1T", "03", "PE"), ("a", "11", "S"), ("c", "02", "V"), ("S1", "12", "PE"), ("S1", "13", "PE"),
+    ("a", "12", "S"), ("st", "a102", "SP"), ("c", "03", "V"), ("S2", "00", "PE"), ("S2", "01", "PE"),
+    ("a", "13", "S"), ("Q", "y01", "V"), ("1T", "04", "PE"), ("d", "00", "V"), ("1T", "05", "PE"),
+    ("c", "04", "S"), ("st", "a122", "SP"), ("S2", "02", "PE"), ("d", "01", "V"), ("S2", "03", "PE"),
+    ("c", "05", "S"), ("1T", "06", "PE"), ("st", "d002", "SP"), ("1T", "07", "PE"), ("c", "06", "S"),
+    ("Q", "y02", "V"), ("d", "02", "V"), ("c", "07", "S"), ("S2", "04", "PE"), ("d", "03", "V"),
+    ("S2", "05", "PE"), ("1T", "10", "PE"), ("Q", "y03", "V"), ("st", "d022", "SP"), ("1T", "11", "PE"),
+    ("c", "10", "S"), ("d", "04", "V"), ("S1", "14", "PE"), ("S1", "15", "PE"), ("c", "11", "S"),
+    ("d", "05", "V"), ("S2", "06", "PE"), ("S2", "07", "PE"), ("a", "14", "S"), ("Q", "y10", "V"),
+    ("st", "d042", "SP"), ("1T", "12", "PE"), ("d", "06", "V"), ("a", "15", "S"), ("1T", "13", "PE"),
+    ("S2", "10", "PE"), ("d", "07", "V"), ("c", "12", "S"), ("S2", "11", "PE"), ("st", "a142", "SP"),
+    ("1T", "14", "PE"), ("st", "d062", "SP"), ("c", "13", "S"), ("1T", "15", "PE"), ("c", "14", "S"),
+    ("Q", "y11", "V"), ("d", "10", "V"), ("c", "15", "S"), ("S2", "12", "PE"), ("d", "11", "V"),
+    ("S2", "13", "PE"), ("1T", "16", "PE"), ("Q", "y12", "V"), ("st", "d102", "SP"), ("1T", "17", "PE"),
+    ("c", "16", "S"), ("d", "12", "V"), ("S1", "16", "PE"), ("S1", "17", "PE"), ("c", "17", "S"),
+    ("d", "13", "V"), ("S2", "14", "PE"), ("S2", "15", "PE"), ("a", "16", "S"), ("Q", "y13", "V"),
+    ("st", "d122", "SP"), ("d", "14", "V"), ("a", "17", "S"), ("S2", "16", "PE"), ("d", "15", "V"),
+    ("S2", "17", "PE"), ("st", "a162", "SP"), ("d", "16", "V"), ("st", "d142", "SP"), ("d", "17", "V"),
+    ("st", "d161", "SP"), ("st", "d171", "SP"),
+)
+
+
+def tile_dcgrucell_pa_kernel(tc, x, support0, support1, out):
+    nc = tc.nc
+    supports = [support0, support1]
+    with ExitStack() as ctx:
+        keep = ctx.enter_context(tc.tile_pool(name="keep", bufs=1))
+        psum = ctx.enter_context(tc.psum_pool(name="psum", bufs=8))
+
+        a_sb = [keep.tile([P, 2048], BF16, name="a_sb%d" % s) for s in range(2)]
+        x_sb = keep.tile([P, 4096], BF16, name="x_sb")
+        ident = keep.tile([P, P], F32, name="ident")
+        a_grp = [keep.tile([P, 2048], BF16, name="a_grp%d" % s, align_bytes=64) for s in range(2)]
+        x_grp = keep.tile([P, 4096], BF16, name="x_grp", align_bytes=64)
+        y_grp = [keep.tile([P, 4096], BF16, name="y_grp%d" % s, align_bytes=64) for s in range(2)]
+        a_codes = [keep.tile([P, 512], U32, name="a_codes%d" % s, align_bytes=64) for s in range(2)]
+        a_scales = [keep.tile([P, 512], U8, name="a_scales%d" % s, align_bytes=64) for s in range(2)]
+        x_codes = keep.tile([P, 1024], U32, name="x_codes", align_bytes=64)
+        x_scales = keep.tile([P, 1024], U8, name="x_scales", align_bytes=64)
+        y_codes = [keep.tile([P, 1024], U32, name="y_codes%d" % s, align_bytes=64) for s in range(2)]
+        y_scales = [keep.tile([P, 1024], U8, name="y_scales%d" % s, align_bytes=64) for s in range(2)]
+        o_sb = [[[keep.tile([P, 2048], F32, name="o_%d_%d_%d" % (kind, s, b)) for b in range(2)]
+                 for s in range(2)] for kind in range(2)]
+
+        make_identity(nc, ident[:])
+        if MANUAL:
+            ctx.enter_context(tc.manual_schedule())
+
+        def load(name):
+            if name[0] == "a":
+                s = int(name[1])
+                dst = a_sb[s][:].rearrange("p (u e m) -> p u e m", u=2, e=2)
+                src = supports[s].rearrange("(u p e) m -> p u e m", u=2, e=2)
+                if len(name) == 3:
+                    e = int(name[2])
+                    nc.sync.dma_start(out=dst[:, :, e, :], in_=src[:, :, e, :])
+                else:
+                    nc.sync.dma_start(
+                        out=a_sb[s][:].rearrange("p (u f) -> p u f", u=2),
+                        in_=supports[s].rearrange("(u p e) m -> p u (e m)", u=2, e=2),
+                    )
+            elif name[1] == "b":
+                b = int(name[2])
+                nc.sync.dma_start(out=x_sb[:, 2048 * b : 2048 * b + 2048],
+                                  in_=x[b].rearrange("(p i) m -> p (i m)", i=4))
+            else:
+                m = int(name[1])
+                b, h = m // 2, m % 2
+                nc.sync.dma_start(
+                    out=x_sb[:, 1024 * m : 1024 * m + 1024].rearrange("p (i m) -> p i m", i=2),
+                    in_=x[b].rearrange("(p i) m -> p i m", i=4)[:, 2 * h : 2 * h + 2, :],
+                )
+
+        def copy_out(eng, dst, src):
+            if eng == "V":
+                nc.vector.tensor_copy(out=dst, in_=src)
+            else:
+                nc.scalar.copy(out=dst, in_=src)
+
+        def quantise(grp, codes, scales, c0, cols):
+            nc.vector.quantize_mx(
+                out=codes[:, c0 : c0 + cols].bitcast(FP8X4),
+                scales=scales[:, c0 : c0 + cols],
+                in_=grp[:, 4 * c0 : 4 * (c0 + cols)],
+            )
+
+        def operand(name):
+            k = int(name[-1])
+            if name[0] == "a":
+                s = int(name[1])
+                return a_sb[s][:].bitcast(F32), [k, 2 + k], a_grp[s], a_codes[s], a_scales[s], 256 * k
+            return x_sb[:].bitcast(F32), [2 * k, 2 * k + 1], x_grp, x_codes, x_scales, 256 * k
+
+        def mx(dst, l_codes, l_scales, l0, r_codes, r_scales, r0, n):
+            nc.tensor.matmul_mx(
+                out=dst,
+                lhsT=l_codes[:, l0 : l0 + P].bitcast(FP8X4),
+                lhsT_scale=l_scales[:, l0 : l0 + P],
+                rhs=r_codes[:, r0 : r0 + n].bitcast(FP8X4),
+                rhs_scale=r_scales[:, r0 : r0 + n],
+                start=True,
+                stop=True,
+            )
+
+        def natural(ap):
+            return ap.rearrange("p (q e) -> p q e", e=2)
+
+        def split_even_odd(ap):
+            return ap.rearrange("p (e q) -> p q e", e=2)
+
+        banks = {}
+        for kind, name, eng in ORDER:
+            if kind == "L":
+                load(name)
+                continue
+            if kind == "st":
+                k0, s, j0, cnt = name[0], int(name[1]), int(name[2]), int(name[3])
+                b, i0 = j0 // 4, j0 % 4
+                kk = 0 if k0 == "a" else 1
+                seg = 2 * s + kk
+                nc.sync.dma_start(
+                    out=out[b, 512 * seg : 512 * seg + 512, :].rearrange("(p i) n -> p i n", i=4)[:, i0 : i0 + cnt, :],
+                    in_=o_sb[kk][s][b][:, 512 * i0 : 512 * (i0 + cnt)].rearrange("p (i n) -> p i n", i=cnt),
+                )
+                continue
+            if kind == "T":
+                words, row_tiles, grp, codes, scales, c0 = operand(name)
+                bank = psum.tile([P, 512], F32, name="bank")
+                for k, rt in enumerate(row_tiles):
+                    for w in range(2):
+                        nc.tensor.transpose(
+                            bank[:, 256 * w + P * k : 256 * w + P * k + P],
+                            words[:, 256 * rt + P * w : 256 * rt + P * w + P],
+                            ident[:],
+                        )
+                banks[(kind, name)] = bank
+                continue
+            if kind == "E":
+                words, row_tiles, grp, codes, scales, c0 = operand(name)
+                copy_out(
+                    eng,
+                    grp[:].bitcast(F32)[:, 2 * c0 : 2 * c0 + 512].rearrange("p (c w) -> p c w", w=2),
+                    banks[("T", name)][:].rearrange("p (w c) -> p c w", w=2),
+                )
+                continue
+            if kind == "Q":
+                if name[0] == "y":
+                    s, m = int(name[1]), int(name[2])
+                    quantise(y_grp[s], y_codes[s], y_scales[s], 256 * m, 256)
+                else:
+                    words, row_tiles, grp, codes, scales, c0 = operand(name)
+                    quantise(grp, codes, scales, c0, 256)
+                continue
+            s, j = int(name[0]), int(name[1])
+            b, i = j // 4, j % 4
+            if kind == "S1":
+                bank = psum.tile([P, 512], F32, name="bank")
+                mx(bank[:], x_codes, x_scales, P * j, a_codes[s], a_scales[s], 0, 512)
+                banks[(kind, name)] = bank
+            elif kind == "1T":
+                bank = psum.tile([P, 512], F32, name="bank")
+                for t in range(4):
+                    mx(bank[:, P * t : P * t + P], a_codes[s], a_scales[s], 256 * (t % 2) + P * (t // 2),
+                       x_codes, x_scales, P * j, P)
+                banks[(kind, name)] = bank
+            elif kind == "S2":
+                bank = psum.tile([P, 512], F32, name="bank")
+                mx(bank[:], y_codes[s], y_scales[s], P * j, a_codes[s], a_scales[s], 0, 512)
+                banks[(kind, name)] = bank
+            elif kind == "a":
+                copy_out(eng, natural(o_sb[0][s][b][:, 512 * i : 512 * i + 512]),
+                         split_even_odd(banks[("S1", name)][:]))
+            elif kind == "c":
+                copy_out(
+                    eng,
+                    y_grp[s][:, 512 * j : 512 * j + 512].rearrange("p (r t) -> p r t", t=4),
+                    banks[("1T", name)][:].rearrange("p (t r) -> p r t", t=4),
+                )
+            elif kind == "d":
+                nc.vector.scalar_tensor_tensor(
+                    out=natural(o_sb[1][s][b][:, 512 * i : 512 * i + 512]),
+                    in0=split_even_odd(banks[("S2", name)][:]),
+                    scalar=2.0,
+                    in1=natural(x_sb[:, 512 * j : 512 * j + 512]),
+                    op0=MULT,
+                    op1=SUB,
+                )

@@ -9,44 +9,11 @@ U32 = mybir.dt.uint32
 U8 = mybir.dt.uint8
 FP8X4 = mybir.dt.float8_e4m3fn_x4
 MULT = mybir.AluOpType.mult
-SUB = mybir.AluOpType.subtract
-P = 128
-FLOPS = 4 * 2 * 1024 * 512 * 512
-MANUAL = True
+SUBTRACT = mybir.AluOpType.subtract
 
-ORDER = (
-    ("L", "a00", "SP"), ("L", "a01", "SP"), ("L", "x0", "SP"), ("L", "x1", "SP"), ("L", "xb1", "SP"),
-    ("L", "a1", "SP"), ("T", "a00", "PE"), ("T", "a01", "PE"), ("E", "a00", "V"), ("T", "x0", "PE"),
-    ("E", "a01", "S"), ("Q", "a00", "V"), ("T", "x1", "PE"), ("E", "x0", "S"), ("Q", "a01", "V"),
-    ("E", "x1", "S"), ("Q", "x0", "V"), ("Q", "x1", "V"), ("S1", "00", "PE"), ("S1", "01", "PE"),
-    ("a", "00", "S"), ("T", "x2", "PE"), ("a", "01", "S"), ("st", "a001", "SP"), ("S1", "02", "PE"),
-    ("E", "x2", "V"), ("S1", "03", "PE"), ("a", "02", "S"), ("st", "a011", "SP"), ("T", "x3", "PE"),
-    ("Q", "x2", "V"), ("a", "03", "S"), ("T", "a10", "PE"), ("E", "x3", "V"), ("st", "a022", "SP"),
-    ("S1", "04", "PE"), ("Q", "x3", "V"), ("S1", "05", "PE"), ("a", "04", "S"), ("E", "a10", "V"),
-    ("T", "a11", "PE"), ("a", "05", "S"), ("Q", "a10", "V"), ("S1", "06", "PE"), ("E", "a11", "V"),
-    ("S1", "07", "PE"), ("a", "06", "S"), ("st", "a042", "SP"), ("1T", "00", "PE"), ("Q", "a11", "V"),
-    ("1T", "01", "PE"), ("a", "07", "S"), ("c", "00", "V"), ("S1", "10", "PE"), ("c", "01", "V"),
-    ("st", "a062", "SP"), ("S1", "11", "PE"), ("a", "10", "S"), ("1T", "02", "PE"), ("Q", "y00", "V"),
-    ("1T", "03", "PE"), ("a", "11", "S"), ("c", "02", "V"), ("S1", "12", "PE"), ("S1", "13", "PE"),
-    ("a", "12", "S"), ("st", "a102", "SP"), ("c", "03", "V"), ("S2", "00", "PE"), ("S2", "01", "PE"),
-    ("a", "13", "S"), ("Q", "y01", "V"), ("1T", "04", "PE"), ("d", "00", "V"), ("1T", "05", "PE"),
-    ("c", "04", "S"), ("st", "a122", "SP"), ("S2", "02", "PE"), ("d", "01", "V"), ("S2", "03", "PE"),
-    ("c", "05", "S"), ("1T", "06", "PE"), ("st", "d002", "SP"), ("1T", "07", "PE"), ("c", "06", "S"),
-    ("Q", "y02", "V"), ("d", "02", "V"), ("c", "07", "S"), ("S2", "04", "PE"), ("d", "03", "V"),
-    ("S2", "05", "PE"), ("1T", "10", "PE"), ("Q", "y03", "V"), ("st", "d022", "SP"), ("1T", "11", "PE"),
-    ("c", "10", "S"), ("d", "04", "V"), ("S1", "14", "PE"), ("S1", "15", "PE"), ("c", "11", "S"),
-    ("d", "05", "V"), ("S2", "06", "PE"), ("S2", "07", "PE"), ("a", "14", "S"), ("Q", "y10", "V"),
-    ("st", "d042", "SP"), ("1T", "12", "PE"), ("d", "06", "V"), ("a", "15", "S"), ("1T", "13", "PE"),
-    ("S2", "10", "PE"), ("d", "07", "V"), ("c", "12", "S"), ("S2", "11", "PE"), ("st", "a142", "SP"),
-    ("1T", "14", "PE"), ("st", "d062", "SP"), ("c", "13", "S"), ("1T", "15", "PE"), ("c", "14", "S"),
-    ("Q", "y11", "V"), ("d", "10", "V"), ("c", "15", "S"), ("S2", "12", "PE"), ("d", "11", "V"),
-    ("S2", "13", "PE"), ("1T", "16", "PE"), ("Q", "y12", "V"), ("st", "d102", "SP"), ("1T", "17", "PE"),
-    ("c", "16", "S"), ("d", "12", "V"), ("S1", "16", "PE"), ("S1", "17", "PE"), ("c", "17", "S"),
-    ("d", "13", "V"), ("S2", "14", "PE"), ("S2", "15", "PE"), ("a", "16", "S"), ("Q", "y13", "V"),
-    ("st", "d122", "SP"), ("d", "14", "V"), ("a", "17", "S"), ("S2", "16", "PE"), ("d", "15", "V"),
-    ("S2", "17", "PE"), ("st", "a162", "SP"), ("d", "16", "V"), ("st", "d142", "SP"), ("d", "17", "V"),
-    ("st", "d161", "SP"), ("st", "d171", "SP"),
-)
+P = 128
+NODES = 512
+FLOPS = 4 * 2 * 1024 * NODES * NODES
 
 
 def tile_dcgrucell_pa_kernel(tc, x, support0, support1, out):
@@ -55,70 +22,69 @@ def tile_dcgrucell_pa_kernel(tc, x, support0, support1, out):
     with ExitStack() as ctx:
         keep = ctx.enter_context(tc.tile_pool(name="keep", bufs=1))
         psum = ctx.enter_context(tc.psum_pool(name="psum", bufs=8))
+        ctx.enter_context(tc.manual_schedule())
 
-        a_sb = [keep.tile([P, 2048], BF16, name="a_sb%d" % s) for s in range(2)]
-        x_sb = keep.tile([P, 4096], BF16, name="x_sb")
+        a_sb = [keep.tile([P, 4 * NODES], BF16, name="a_sb%d" % s) for s in range(2)]
+        x_sb = keep.tile([P, 8 * NODES], BF16, name="x_sb")
         ident = keep.tile([P, P], F32, name="ident")
-        a_grp = [keep.tile([P, 2048], BF16, name="a_grp%d" % s, align_bytes=64) for s in range(2)]
-        x_grp = keep.tile([P, 4096], BF16, name="x_grp", align_bytes=64)
-        y_grp = [keep.tile([P, 4096], BF16, name="y_grp%d" % s, align_bytes=64) for s in range(2)]
-        a_codes = [keep.tile([P, 512], U32, name="a_codes%d" % s, align_bytes=64) for s in range(2)]
-        a_scales = [keep.tile([P, 512], U8, name="a_scales%d" % s, align_bytes=64) for s in range(2)]
+        a_grp = [keep.tile([P, 4 * NODES], BF16, name="a_grp%d" % s, align_bytes=64) for s in range(2)]
+        x_grp = keep.tile([P, 4 * 1024], BF16, name="x_grp", align_bytes=64)
+        y_grp = [keep.tile([P, 4 * 1024], BF16, name="y_grp%d" % s, align_bytes=64) for s in range(2)]
+        a_codes = [keep.tile([P, NODES], U32, name="a_codes%d" % s, align_bytes=64) for s in range(2)]
+        a_scales = [keep.tile([P, NODES], U8, name="a_scales%d" % s, align_bytes=64) for s in range(2)]
         x_codes = keep.tile([P, 1024], U32, name="x_codes", align_bytes=64)
         x_scales = keep.tile([P, 1024], U8, name="x_scales", align_bytes=64)
         y_codes = [keep.tile([P, 1024], U32, name="y_codes%d" % s, align_bytes=64) for s in range(2)]
         y_scales = [keep.tile([P, 1024], U8, name="y_scales%d" % s, align_bytes=64) for s in range(2)]
-        o_sb = [[[keep.tile([P, 2048], F32, name="o_%d_%d_%d" % (kind, s, b)) for b in range(2)]
-                 for s in range(2)] for kind in range(2)]
+        o_sb = [[keep.tile([P, 4 * NODES], F32, name="o_sb%d_%d" % (seg, b)) for b in range(2)] for seg in range(4)]
 
+        a_rows = [a.rearrange("(u p e) m -> p u e m", u=2, e=2) for a in supports]
+        a_dst = [t[:].rearrange("p (u e m) -> p u e m", u=2, e=2) for t in a_sb]
+        for e in range(2):
+            nc.sync.dma_start(out=a_dst[0][:, :, e, :], in_=a_rows[0][:, :, e, :])
+        for h in range(2):
+            nc.sync.dma_start(
+                out=x_sb[:, 1024 * h : 1024 * h + 1024].rearrange("p (i m) -> p i m", i=2),
+                in_=x[0].rearrange("(p i) m -> p i m", i=4)[:, 2 * h : 2 * h + 2, :],
+            )
+        nc.sync.dma_start(out=x_sb[:, 2048:4096], in_=x[1].rearrange("(p i) m -> p (i m)", i=4))
+        nc.sync.dma_start(
+            out=a_sb[1][:].rearrange("p (u f) -> p u f", u=2),
+            in_=support1.rearrange("(u p e) m -> p u (e m)", u=2, e=2),
+        )
         make_identity(nc, ident[:])
-        if MANUAL:
-            ctx.enter_context(tc.manual_schedule())
 
-        def load(name):
-            if name[0] == "a":
-                s = int(name[1])
-                dst = a_sb[s][:].rearrange("p (u e m) -> p u e m", u=2, e=2)
-                src = supports[s].rearrange("(u p e) m -> p u e m", u=2, e=2)
-                if len(name) == 3:
-                    e = int(name[2])
-                    nc.sync.dma_start(out=dst[:, :, e, :], in_=src[:, :, e, :])
-                else:
-                    nc.sync.dma_start(
-                        out=a_sb[s][:].rearrange("p (u f) -> p u f", u=2),
-                        in_=supports[s].rearrange("(u p e) m -> p u (e m)", u=2, e=2),
-                    )
-            elif name[1] == "b":
-                b = int(name[2])
-                nc.sync.dma_start(out=x_sb[:, 2048 * b : 2048 * b + 2048],
-                                  in_=x[b].rearrange("(p i) m -> p (i m)", i=4))
-            else:
-                m = int(name[1])
-                b, h = m // 2, m % 2
-                nc.sync.dma_start(
-                    out=x_sb[:, 1024 * m : 1024 * m + 1024].rearrange("p (i m) -> p i m", i=2),
-                    in_=x[b].rearrange("(p i) m -> p i m", i=4)[:, 2 * h : 2 * h + 2, :],
-                )
-
-        def copy_out(eng, dst, src):
-            if eng == "V":
+        def copy_out(engine, dst, src):
+            if engine is nc.vector:
                 nc.vector.tensor_copy(out=dst, in_=src)
             else:
                 nc.scalar.copy(out=dst, in_=src)
 
-        def quantise(grp, codes, scales, c0, cols):
-            nc.vector.quantize_mx(
-                out=codes[:, c0 : c0 + cols].bitcast(FP8X4),
-                scales=scales[:, c0 : c0 + cols],
-                in_=grp[:, 4 * c0 : 4 * (c0 + cols)],
+        def transpose_pair(src, row_tiles):
+            words = src[:].bitcast(F32)
+            bank = psum.tile([P, 512], F32, name="bank")
+            for k, rt in enumerate(row_tiles):
+                for w in range(2):
+                    nc.tensor.transpose(
+                        bank[:, 256 * w + P * k : 256 * w + P * k + P],
+                        words[:, 256 * rt + P * w : 256 * rt + P * w + P],
+                        ident[:],
+                    )
+            return bank
+
+        def regroup(engine, bank, grp, c0):
+            copy_out(
+                engine,
+                grp[:].bitcast(F32)[:, 2 * c0 : 2 * c0 + 512].rearrange("p (c w) -> p c w", w=2),
+                bank[:].rearrange("p (w c) -> p c w", w=2),
             )
 
-        def operand(name):
-            k = int(name[-1])
-            if name[0] == "a":
-                s = int(name[1])
-                return a_sb[s][:].bitcast(F32), [k, 2 + k], a_grp[s], a_codes[s], a_scales[s], 256 * k
-            return x_sb[:].bitcast(F32), [2 * k, 2 * k + 1], x_grp, x_codes, x_scales, 256 * k
+        def quantise(grp, codes, scales, c0):
+            nc.vector.quantize_mx(
+                out=codes[:, c0 : c0 + 256].bitcast(FP8X4),
+                scales=scales[:, c0 : c0 + 256],
+                in_=grp[:, 4 * c0 : 4 * c0 + 1024],
+            )
 
         def mx(dst, l_codes, l_scales, l0, r_codes, r_scales, r0, n):
             nc.tensor.matmul_mx(
@@ -131,86 +97,124 @@ def tile_dcgrucell_pa_kernel(tc, x, support0, support1, out):
                 stop=True,
             )
 
-        def natural(ap):
-            return ap.rearrange("p (q e) -> p q e", e=2)
-
-        def split_even_odd(ap):
-            return ap.rearrange("p (e q) -> p q e", e=2)
-
-        banks = {}
-        for kind, name, eng in ORDER:
-            if kind == "L":
-                load(name)
-                continue
-            if kind == "st":
-                k0, s, j0, cnt = name[0], int(name[1]), int(name[2]), int(name[3])
-                b, i0 = j0 // 4, j0 % 4
-                kk = 0 if k0 == "a" else 1
-                seg = 2 * s + kk
-                nc.sync.dma_start(
-                    out=out[b, 512 * seg : 512 * seg + 512, :].rearrange("(p i) n -> p i n", i=4)[:, i0 : i0 + cnt, :],
-                    in_=o_sb[kk][s][b][:, 512 * i0 : 512 * (i0 + cnt)].rearrange("p (i n) -> p i n", i=cnt),
-                )
-                continue
-            if kind == "T":
-                words, row_tiles, grp, codes, scales, c0 = operand(name)
+        def rows_by_support(l_codes, l_scales, n):
+            s = n // 4
+            banks = []
+            for j in (2 * (n % 4), 2 * (n % 4) + 1):
                 bank = psum.tile([P, 512], F32, name="bank")
-                for k, rt in enumerate(row_tiles):
-                    for w in range(2):
-                        nc.tensor.transpose(
-                            bank[:, 256 * w + P * k : 256 * w + P * k + P],
-                            words[:, 256 * rt + P * w : 256 * rt + P * w + P],
-                            ident[:],
-                        )
-                banks[(kind, name)] = bank
-                continue
-            if kind == "E":
-                words, row_tiles, grp, codes, scales, c0 = operand(name)
-                copy_out(
-                    eng,
-                    grp[:].bitcast(F32)[:, 2 * c0 : 2 * c0 + 512].rearrange("p (c w) -> p c w", w=2),
-                    banks[("T", name)][:].rearrange("p (w c) -> p c w", w=2),
-                )
-                continue
-            if kind == "Q":
-                if name[0] == "y":
-                    s, m = int(name[1]), int(name[2])
-                    quantise(y_grp[s], y_codes[s], y_scales[s], 256 * m, 256)
-                else:
-                    words, row_tiles, grp, codes, scales, c0 = operand(name)
-                    quantise(grp, codes, scales, c0, 256)
-                continue
-            s, j = int(name[0]), int(name[1])
-            b, i = j // 4, j % 4
-            if kind == "S1":
-                bank = psum.tile([P, 512], F32, name="bank")
-                mx(bank[:], x_codes, x_scales, P * j, a_codes[s], a_scales[s], 0, 512)
-                banks[(kind, name)] = bank
-            elif kind == "1T":
+                mx(bank[:], l_codes, l_scales, P * j, a_codes[s], a_scales[s], 0, NODES)
+                banks.append(bank)
+            return banks
+
+        def x1_passes(n):
+            return rows_by_support(x_codes, x_scales, n)
+
+        def x2_passes(n):
+            return rows_by_support(y_codes[n // 4], y_scales[n // 4], n)
+
+        def x1t_passes(n):
+            s = n // 4
+            banks = []
+            for j in (2 * (n % 4), 2 * (n % 4) + 1):
                 bank = psum.tile([P, 512], F32, name="bank")
                 for t in range(4):
                     mx(bank[:, P * t : P * t + P], a_codes[s], a_scales[s], 256 * (t % 2) + P * (t // 2),
                        x_codes, x_scales, P * j, P)
-                banks[(kind, name)] = bank
-            elif kind == "S2":
-                bank = psum.tile([P, 512], F32, name="bank")
-                mx(bank[:], y_codes[s], y_scales[s], P * j, a_codes[s], a_scales[s], 0, 512)
-                banks[(kind, name)] = bank
-            elif kind == "a":
-                copy_out(eng, natural(o_sb[0][s][b][:, 512 * i : 512 * i + 512]),
-                         split_even_odd(banks[("S1", name)][:]))
-            elif kind == "c":
+                banks.append(bank)
+            return banks
+
+        def natural(ap):
+            return ap.rearrange("p (q e) -> p q e", e=2)
+
+        def even_odd(ap):
+            return ap.rearrange("p (e q) -> p q e", e=2)
+
+        def store(seg, m, first, count):
+            b, i0 = m // 2, 2 * (m % 2) + first
+            nc.sync.dma_start(
+                out=out[b, 512 * seg : 512 * seg + 512, :].rearrange("(p i) n -> p i n", i=4)[:, i0 : i0 + count, :],
+                in_=o_sb[seg][b][:, 512 * i0 : 512 * (i0 + count)].rearrange("p (i n) -> p i n", i=count),
+            )
+
+        def x1_out(n, banks, tile_by_tile=False):
+            seg, m = 2 * (n // 4), n % 4
+            for k in range(2):
+                i = 2 * (m % 2) + k
+                nc.scalar.copy(out=natural(o_sb[seg][m // 2][:, 512 * i : 512 * i + 512]), in_=even_odd(banks[k][:]))
+                if tile_by_tile:
+                    store(seg, m, k, 1)
+            if not tile_by_tile:
+                store(seg, m, 0, 2)
+
+        def x1t_out(engine, n, banks):
+            s, m = n // 4, n % 4
+            for k in range(2):
+                j = 2 * m + k
                 copy_out(
-                    eng,
+                    engine,
                     y_grp[s][:, 512 * j : 512 * j + 512].rearrange("p (r t) -> p r t", t=4),
-                    banks[("1T", name)][:].rearrange("p (t r) -> p r t", t=4),
+                    banks[k][:].rearrange("p (t r) -> p r t", t=4),
                 )
-            elif kind == "d":
+
+        def quantise_x1t(n):
+            s = n // 4
+            quantise(y_grp[s], y_codes[s], y_scales[s], 256 * (n % 4))
+
+        def x2_out(n, banks, tile_by_tile=False):
+            seg, m = 2 * (n // 4) + 1, n % 4
+            for k in range(2):
+                i = 2 * (m % 2) + k
+                j = 2 * m + k
                 nc.vector.scalar_tensor_tensor(
-                    out=natural(o_sb[1][s][b][:, 512 * i : 512 * i + 512]),
-                    in0=split_even_odd(banks[("S2", name)][:]),
+                    out=natural(o_sb[seg][m // 2][:, 512 * i : 512 * i + 512]),
+                    in0=even_odd(banks[k][:]),
                     scalar=2.0,
                     in1=natural(x_sb[:, 512 * j : 512 * j + 512]),
                     op0=MULT,
-                    op1=SUB,
+                    op1=SUBTRACT,
                 )
+                if tile_by_tile:
+                    store(seg, m, k, 1)
+            if not tile_by_tile:
+                store(seg, m, 0, 2)
+
+        a_banks = [transpose_pair(a_sb[0], [e, 2 + e]) for e in range(2)]
+        x_banks = [transpose_pair(x_sb, [2 * m, 2 * m + 1]) for m in range(4)]
+        regroup(nc.vector, a_banks[0], a_grp[0], 0)
+        regroup(nc.scalar, a_banks[1], a_grp[0], 256)
+        for e in range(2):
+            quantise(a_grp[0], a_codes[0], a_scales[0], 256 * e)
+        for m in range(3):
+            regroup(nc.scalar, x_banks[m], x_grp, 256 * m)
+            quantise(x_grp, x_codes, x_scales, 256 * m)
+        regroup(nc.vector, x_banks[3], x_grp, 768)
+        quantise(x_grp, x_codes, x_scales, 768)
+
+        for n in range(4):
+            b1 = x1_passes(n)
+            if n < 2:
+                bt = x1t_passes(n)
+            if n == 2:
+                a_banks = [transpose_pair(a_sb[1], [e, 2 + e]) for e in range(2)]
+            x1_out(n, b1, tile_by_tile=(n == 0))
+            if n < 2:
+                x1t_out(nc.vector, n, bt)
+                quantise_x1t(n)
+        for e in range(2):
+            regroup(nc.vector, a_banks[e], a_grp[1], 256 * e)
+            quantise(a_grp[1], a_codes[1], a_scales[1], 256 * e)
+
+        for k in range(3):
+            for h in range(2):
+                bt = x1t_passes(2 + 2 * k + h)
+                b2 = x2_passes(2 * k + h)
+                x1t_out(nc.scalar, 2 + 2 * k + h, bt)
+                x2_out(2 * k + h, b2)
+                quantise_x1t(2 + 2 * k + h)
+            b1 = x1_passes(4 + k)
+            x1_out(4 + k, b1)
+        b1 = x1_passes(7)
+        b2 = [x2_passes(6), x2_passes(7)]
+        x2_out(6, b2[0])
+        x1_out(7, b1)
+        x2_out(7, b2[1], tile_by_tile=True)

@@ -40,14 +40,16 @@ def tile_dcgrucell_pa_kernel(tc, x, support0, support1, out):
 
         a_rows = [a.rearrange("(u p e) m -> p u e m", u=2, e=2) for a in supports]
         a_dst = [t[:].rearrange("p (u e m) -> p u e m", u=2, e=2) for t in a_sb]
+        x_rows = [x[b].rearrange("(p i) m -> p i m", i=4) for b in range(2)]
+        x_dst = x_sb[:].rearrange("p (j m) -> p j m", j=8)
         for e in range(2):
-            nc.sync.dma_start(out=a_dst[0][:, :, e, :], in_=a_rows[0][:, :, e, :])
-        for h in range(2):
-            nc.sync.dma_start(
-                out=x_sb[:, 1024 * h : 1024 * h + 1024].rearrange("p (i m) -> p i m", i=2),
-                in_=x[0].rearrange("(p i) m -> p i m", i=4)[:, 2 * h : 2 * h + 2, :],
-            )
-        nc.sync.dma_start(out=x_sb[:, 2048:4096], in_=x[1].rearrange("(p i) m -> p (i m)", i=4))
+            for u in range(2):
+                nc.sync.dma_start(out=a_dst[0][:, u, e, :], in_=a_rows[0][:, u, e, :])
+        for i in range(2):
+            nc.sync.dma_start(out=x_dst[:, i, :], in_=x_rows[0][:, i, :])
+        for m in range(1, 4):
+            nc.sync.dma_start(out=x_dst[:, 2 * m : 2 * m + 2, :],
+                              in_=x_rows[m // 2][:, 2 * (m % 2) : 2 * (m % 2) + 2, :])
         nc.sync.dma_start(
             out=a_sb[1][:].rearrange("p (u f) -> p u f", u=2),
             in_=support1.rearrange("(u p e) m -> p u (e m)", u=2, e=2),
@@ -63,27 +65,28 @@ def tile_dcgrucell_pa_kernel(tc, x, support0, support1, out):
         def transpose_pair(src, row_tiles):
             words = src[:].bitcast(F32)
             bank = psum.tile([P, 512], F32, name="bank")
+            cols = P * len(row_tiles)
             for k, rt in enumerate(row_tiles):
                 for w in range(2):
                     nc.tensor.transpose(
-                        bank[:, 256 * w + P * k : 256 * w + P * k + P],
+                        bank[:, cols * w + P * k : cols * w + P * k + P],
                         words[:, 256 * rt + P * w : 256 * rt + P * w + P],
                         ident[:],
                     )
             return bank
 
-        def regroup(engine, bank, grp, c0):
+        def regroup(engine, bank, grp, c0, cols=256):
             copy_out(
                 engine,
-                grp[:].bitcast(F32)[:, 2 * c0 : 2 * c0 + 512].rearrange("p (c w) -> p c w", w=2),
-                bank[:].rearrange("p (w c) -> p c w", w=2),
+                grp[:].bitcast(F32)[:, 2 * c0 : 2 * (c0 + cols)].rearrange("p (c w) -> p c w", w=2),
+                bank[:, 0 : 2 * cols].rearrange("p (w c) -> p c w", w=2),
             )
 
-        def quantise(grp, codes, scales, c0):
+        def quantise(grp, codes, scales, c0, cols=256):
             nc.vector.quantize_mx(
-                out=codes[:, c0 : c0 + 256].bitcast(FP8X4),
-                scales=scales[:, c0 : c0 + 256],
-                in_=grp[:, 4 * c0 : 4 * c0 + 1024],
+                out=codes[:, c0 : c0 + cols].bitcast(FP8X4),
+                scales=scales[:, c0 : c0 + cols],
+                in_=grp[:, 4 * c0 : 4 * (c0 + cols)],
             )
 
         def mx(dst, l_codes, l_scales, l0, r_codes, r_scales, r0, n):
@@ -178,17 +181,22 @@ def tile_dcgrucell_pa_kernel(tc, x, support0, support1, out):
             if not tile_by_tile:
                 store(seg, m, 0, 2)
 
-        a_banks = [transpose_pair(a_sb[0], [e, 2 + e]) for e in range(2)]
-        x_banks = [transpose_pair(x_sb, [2 * m, 2 * m + 1]) for m in range(4)]
-        regroup(nc.vector, a_banks[0], a_grp[0], 0)
-        regroup(nc.scalar, a_banks[1], a_grp[0], 256)
-        for e in range(2):
-            quantise(a_grp[0], a_codes[0], a_scales[0], 256 * e)
-        for m in range(3):
-            regroup(nc.scalar, x_banks[m], x_grp, 256 * m)
+        a_banks = [transpose_pair(a_sb[0], [2 * u + e]) for e in range(2) for u in range(2)]
+        x_banks = [transpose_pair(x_sb, [j]) for j in range(2)]
+        x_banks.append(transpose_pair(x_sb, [2, 3]))
+        for k in range(4):
+            c0 = 256 * (k // 2) + P * (k % 2)
+            regroup(nc.vector if k == 0 else nc.scalar, a_banks[k], a_grp[0], c0, P)
+            quantise(a_grp[0], a_codes[0], a_scales[0], c0, P)
+        for j in range(2):
+            regroup(nc.scalar, x_banks[j], x_grp, P * j, P)
+            quantise(x_grp, x_codes, x_scales, P * j, P)
+        regroup(nc.scalar, x_banks[2], x_grp, 256)
+        quantise(x_grp, x_codes, x_scales, 256)
+        x_banks = [transpose_pair(x_sb, [2 * m, 2 * m + 1]) for m in (2, 3)]
+        for m in (2, 3):
+            regroup(nc.scalar if m == 2 else nc.vector, x_banks[m - 2], x_grp, 256 * m)
             quantise(x_grp, x_codes, x_scales, 256 * m)
-        regroup(nc.vector, x_banks[3], x_grp, 768)
-        quantise(x_grp, x_codes, x_scales, 768)
 
         for n in range(4):
             b1 = x1_passes(n)

@@ -40,16 +40,14 @@ def tile_dcgrucell_pa_kernel(tc, x, support0, support1, out):
 
         a_rows = [a.rearrange("(u p e) m -> p u e m", u=2, e=2) for a in supports]
         a_dst = [t[:].rearrange("p (u e m) -> p u e m", u=2, e=2) for t in a_sb]
-        x_rows = [x[b].rearrange("(p i) m -> p i m", i=4) for b in range(2)]
-        x_dst = x_sb[:].rearrange("p (j m) -> p j m", j=8)
         for e in range(2):
-            for u in range(2):
-                nc.sync.dma_start(out=a_dst[0][:, u, e, :], in_=a_rows[0][:, u, e, :])
-        for i in range(2):
-            nc.sync.dma_start(out=x_dst[:, i, :], in_=x_rows[0][:, i, :])
-        for m in range(1, 4):
-            nc.sync.dma_start(out=x_dst[:, 2 * m : 2 * m + 2, :],
-                              in_=x_rows[m // 2][:, 2 * (m % 2) : 2 * (m % 2) + 2, :])
+            nc.sync.dma_start(out=a_dst[0][:, :, e, :], in_=a_rows[0][:, :, e, :])
+        for h in range(2):
+            nc.sync.dma_start(
+                out=x_sb[:, 1024 * h : 1024 * h + 1024].rearrange("p (i m) -> p i m", i=2),
+                in_=x[0].rearrange("(p i) m -> p i m", i=4)[:, 2 * h : 2 * h + 2, :],
+            )
+        nc.sync.dma_start(out=x_sb[:, 2048:4096], in_=x[1].rearrange("(p i) m -> p (i m)", i=4))
         nc.sync.dma_start(
             out=a_sb[1][:].rearrange("p (u f) -> p u f", u=2),
             in_=support1.rearrange("(u p e) m -> p u (e m)", u=2, e=2),
@@ -65,28 +63,27 @@ def tile_dcgrucell_pa_kernel(tc, x, support0, support1, out):
         def transpose_pair(src, row_tiles):
             words = src[:].bitcast(F32)
             bank = psum.tile([P, 512], F32, name="bank")
-            cols = P * len(row_tiles)
             for k, rt in enumerate(row_tiles):
                 for w in range(2):
                     nc.tensor.transpose(
-                        bank[:, cols * w + P * k : cols * w + P * k + P],
+                        bank[:, 256 * w + P * k : 256 * w + P * k + P],
                         words[:, 256 * rt + P * w : 256 * rt + P * w + P],
                         ident[:],
                     )
             return bank
 
-        def regroup(engine, bank, grp, c0, cols=256):
+        def regroup(engine, bank, grp, c0):
             copy_out(
                 engine,
-                grp[:].bitcast(F32)[:, 2 * c0 : 2 * (c0 + cols)].rearrange("p (c w) -> p c w", w=2),
-                bank[:, 0 : 2 * cols].rearrange("p (w c) -> p c w", w=2),
+                grp[:].bitcast(F32)[:, 2 * c0 : 2 * c0 + 512].rearrange("p (c w) -> p c w", w=2),
+                bank[:].rearrange("p (w c) -> p c w", w=2),
             )
 
-        def quantise(grp, codes, scales, c0, cols=256):
+        def quantise(grp, codes, scales, c0):
             nc.vector.quantize_mx(
-                out=codes[:, c0 : c0 + cols].bitcast(FP8X4),
-                scales=scales[:, c0 : c0 + cols],
-                in_=grp[:, 4 * c0 : 4 * (c0 + cols)],
+                out=codes[:, c0 : c0 + 256].bitcast(FP8X4),
+                scales=scales[:, c0 : c0 + 256],
+                in_=grp[:, 4 * c0 : 4 * c0 + 1024],
             )
 
         def mx(dst, l_codes, l_scales, l0, r_codes, r_scales, r0, n):
@@ -181,36 +178,47 @@ def tile_dcgrucell_pa_kernel(tc, x, support0, support1, out):
             if not tile_by_tile:
                 store(seg, m, 0, 2)
 
-        a_banks = [transpose_pair(a_sb[0], [2 * u + e]) for e in range(2) for u in range(2)]
-        x_banks = [transpose_pair(x_sb, [j]) for j in range(2)]
-        x_banks.append(transpose_pair(x_sb, [2, 3]))
-        for k in range(4):
-            c0 = 256 * (k // 2) + P * (k % 2)
-            regroup(nc.vector if k == 0 else nc.scalar, a_banks[k], a_grp[0], c0, P)
-            quantise(a_grp[0], a_codes[0], a_scales[0], c0, P)
-        for j in range(2):
-            regroup(nc.scalar, x_banks[j], x_grp, P * j, P)
-            quantise(x_grp, x_codes, x_scales, P * j, P)
-        regroup(nc.scalar, x_banks[2], x_grp, 256)
-        quantise(x_grp, x_codes, x_scales, 256)
-        x_banks = [transpose_pair(x_sb, [2 * m, 2 * m + 1]) for m in (2, 3)]
-        for m in (2, 3):
-            regroup(nc.scalar if m == 2 else nc.vector, x_banks[m - 2], x_grp, 256 * m)
+        a_banks = [transpose_pair(a_sb[0], [e, 2 + e]) for e in range(2)]
+        x_banks = [transpose_pair(x_sb, [2 * m, 2 * m + 1]) for m in range(4)]
+        regroup(nc.vector, a_banks[0], a_grp[0], 0)
+        regroup(nc.scalar, a_banks[1], a_grp[0], 256)
+        for e in range(2):
+            quantise(a_grp[0], a_codes[0], a_scales[0], 256 * e)
+        for m in range(3):
+            regroup(nc.scalar, x_banks[m], x_grp, 256 * m)
             quantise(x_grp, x_codes, x_scales, 256 * m)
+
+        t_banks = []
+
+        def vector_copy(step):
+            if step == 0:
+                regroup(nc.vector, x_banks[3], x_grp, 768)
+            elif step < 3:
+                x1t_out(nc.vector, step - 1, t_banks[step - 1])
+            else:
+                regroup(nc.vector, a_banks[step - 3], a_grp[1], 256 * (step - 3))
+
+        def vector_quantise(step):
+            if step == 0:
+                quantise(x_grp, x_codes, x_scales, 768)
+            elif step < 3:
+                quantise_x1t(step - 1)
+            else:
+                quantise(a_grp[1], a_codes[1], a_scales[1], 256 * (step - 3))
 
         for n in range(4):
             b1 = x1_passes(n)
             if n < 2:
-                bt = x1t_passes(n)
+                t_banks.append(x1t_passes(n))
             if n == 2:
                 a_banks = [transpose_pair(a_sb[1], [e, 2 + e]) for e in range(2)]
             x1_out(n, b1, tile_by_tile=(n == 0))
-            if n < 2:
-                x1t_out(nc.vector, n, bt)
-                quantise_x1t(n)
-        for e in range(2):
-            regroup(nc.vector, a_banks[e], a_grp[1], 256 * e)
-            quantise(a_grp[1], a_codes[1], a_scales[1], 256 * e)
+            vector_copy(n)
+            if n > 0:
+                vector_quantise(n - 1)
+        vector_copy(4)
+        vector_quantise(3)
+        vector_quantise(4)
 
         for k in range(3):
             for h in range(2):

@@ -212,7 +212,7 @@ def tile_dcgrucell_pa_kernel(tc, x, support0, support1, out):
                 t_banks.append(x1t_passes(n))
             if n == 2:
                 a_banks = [transpose_pair(a_sb[1], [e, 2 + e]) for e in range(2)]
-            x1_out(n, b1, tile_by_tile=(n == 0))
+            x1_out(n, b1, tile_by_tile=True)
             vector_copy(n)
             if n > 0:
                 vector_quantise(n - 1)
@@ -225,12 +225,12 @@ def tile_dcgrucell_pa_kernel(tc, x, support0, support1, out):
                 bt = x1t_passes(2 + 2 * k + h)
                 b2 = x2_passes(2 * k + h)
                 x1t_out(nc.scalar, 2 + 2 * k + h, bt)
-                x2_out(2 * k + h, b2)
+                x2_out(2 * k + h, b2, tile_by_tile=True)
                 quantise_x1t(2 + 2 * k + h)
             b1 = x1_passes(4 + k)
-            x1_out(4 + k, b1)
+            x1_out(4 + k, b1, tile_by_tile=True)
         b1 = x1_passes(7)
         b2 = [x2_passes(6), x2_passes(7)]
-        x2_out(6, b2[0])
-        x1_out(7, b1)
+        x2_out(6, b2[0], tile_by_tile=True)
+        x1_out(7, b1, tile_by_tile=True)
         x2_out(7, b2[1], tile_by_tile=True)

from contextlib import ExitStack

import concourse.mybir as mybir
from concourse.masks import make_identity

F32 = mybir.dt.float32
BF16 = mybir.dt.bfloat16
U32 = mybir.dt.uint32
U8 = mybir.dt.uint8
FP8X4 = mybir.dt.float8_e4m3fn_x4
MULT = mybir.AluOpType.mult
SUBTRACT = mybir.AluOpType.subtract

P = 128
NODES = 512
FLOPS = 4 * 2 * 1024 * NODES * NODES


def tile_dcgrucell_pa_kernel(tc, x, support0, support1, out):
    nc = tc.nc
    supports = [support0, support1]
    with ExitStack() as ctx:
        keep = ctx.enter_context(tc.tile_pool(name="keep", bufs=1))
        psum = ctx.enter_context(tc.psum_pool(name="psum", bufs=8))
        ctx.enter_context(tc.manual_schedule())

        a_sb = [keep.tile([P, 4 * NODES], BF16, name="a_sb%d" % s) for s in range(2)]
        x_sb = keep.tile([P, 8 * NODES], BF16, name="x_sb")
        ident = keep.tile([P, P], F32, name="ident")
        a_grp = [keep.tile([P, 4 * NODES], BF16, name="a_grp%d" % s, align_bytes=64) for s in range(2)]
        x_grp = keep.tile([P, 4 * 1024], BF16, name="x_grp", align_bytes=64)
        y_grp = [keep.tile([P, 4 * 1024], BF16, name="y_grp%d" % s, align_bytes=64) for s in range(2)]
        a_codes = [keep.tile([P, NODES], U32, name="a_codes%d" % s, align_bytes=64) for s in range(2)]
        a_scales = [keep.tile([P, NODES], U8, name="a_scales%d" % s, align_bytes=64) for s in range(2)]
        x_codes = keep.tile([P, 1024], U32, name="x_codes", align_bytes=64)
        x_scales = keep.tile([P, 1024], U8, name="x_scales", align_bytes=64)
        y_codes = [keep.tile([P, 1024], U32, name="y_codes%d" % s, align_bytes=64) for s in range(2)]
        y_scales = [keep.tile([P, 1024], U8, name="y_scales%d" % s, align_bytes=64) for s in range(2)]
        o_sb = [[keep.tile([P, 4 * NODES], F32, name="o_sb%d_%d" % (seg, b)) for b in range(2)] for seg in range(4)]

        a_rows = [a.rearrange("(u p e) m -> p u e m", u=2, e=2) for a in supports]
        a_dst = [t[:].rearrange("p (u e m) -> p u e m", u=2, e=2) for t in a_sb]
        for e in range(2):
            nc.sync.dma_start(out=a_dst[0][:, :, e, :], in_=a_rows[0][:, :, e, :])
        for h in range(2):
            nc.sync.dma_start(
                out=x_sb[:, 1024 * h : 1024 * h + 1024].rearrange("p (i m) -> p i m", i=2),
                in_=x[0].rearrange("(p i) m -> p i m", i=4)[:, 2 * h : 2 * h + 2, :],
            )
        nc.sync.dma_start(out=x_sb[:, 2048:4096], in_=x[1].rearrange("(p i) m -> p (i m)", i=4))
        nc.sync.dma_start(
            out=a_sb[1][:].rearrange("p (u f) -> p u f", u=2),
            in_=support1.rearrange("(u p e) m -> p u (e m)", u=2, e=2),
        )
        make_identity(nc, ident[:])

        def copy_out(engine, dst, src):
            if engine is nc.vector:
                nc.vector.tensor_copy(out=dst, in_=src)
            else:
                nc.scalar.copy(out=dst, in_=src)

        def transpose_pair(src, row_tiles):
            words = src[:].bitcast(F32)
            bank = psum.tile([P, 512], F32, name="bank")
            for k, rt in enumerate(row_tiles):
                for w in range(2):
                    nc.tensor.transpose(
                        bank[:, 256 * w + P * k : 256 * w + P * k + P],
                        words[:, 256 * rt + P * w : 256 * rt + P * w + P],
                        ident[:],
                    )
            return bank

        def regroup(engine, bank, grp, c0):
            copy_out(
                engine,
                grp[:].bitcast(F32)[:, 2 * c0 : 2 * c0 + 512].rearrange("p (c w) -> p c w", w=2),
                bank[:].rearrange("p (w c) -> p c w", w=2),
            )

        def quantise(grp, codes, scales, c0):
            nc.vector.quantize_mx(
                out=codes[:, c0 : c0 + 256].bitcast(FP8X4),
                scales=scales[:, c0 : c0 + 256],
                in_=grp[:, 4 * c0 : 4 * c0 + 1024],
            )

        def mx(dst, l_codes, l_scales, l0, r_codes, r_scales, r0, n):
            nc.tensor.matmul_mx(
                out=dst,
                lhsT=l_codes[:, l0 : l0 + P].bitcast(FP8X4),
                lhsT_scale=l_scales[:, l0 : l0 + P],
                rhs=r_codes[:, r0 : r0 + n].bitcast(FP8X4),
                rhs_scale=r_scales[:, r0 : r0 + n],
                start=True,
                stop=True,
            )

        def rows_by_support(l_codes, l_scales, n):
            s = n // 4
            banks = []
            for j in (2 * (n % 4), 2 * (n % 4) + 1):
                bank = psum.tile([P, 512], F32, name="bank")
                mx(bank[:], l_codes, l_scales, P * j, a_codes[s], a_scales[s], 0, NODES)
                banks.append(bank)
            return banks

        def x1_passes(n):
            return rows_by_support(x_codes, x_scales, n)

        def x2_passes(n):
            return rows_by_support(y_codes[n // 4], y_scales[n // 4], n)

        def x1t_passes(n):
            s = n // 4
            banks = []
            for j in (2 * (n % 4), 2 * (n % 4) + 1):
                bank = psum.tile([P, 512], F32, name="bank")
                for t in range(4):
                    mx(bank[:, P * t : P * t + P], a_codes[s], a_scales[s], 256 * (t % 2) + P * (t // 2),
                       x_codes, x_scales, P * j, P)
                banks.append(bank)
            return banks

        def natural(ap):
            return ap.rearrange("p (q e) -> p q e", e=2)

        def even_odd(ap):
            return ap.rearrange("p (e q) -> p q e", e=2)

        def store(seg, m, first, count):
            b, i0 = m // 2, 2 * (m % 2) + first
            nc.sync.dma_start(
                out=out[b, 512 * seg : 512 * seg + 512, :].rearrange("(p i) n -> p i n", i=4)[:, i0 : i0 + count, :],
                in_=o_sb[seg][b][:, 512 * i0 : 512 * (i0 + count)].rearrange("p (i n) -> p i n", i=count),
            )

        def x1_out(n, banks, tile_by_tile=False):
            seg, m = 2 * (n // 4), n % 4
            for k in range(2):
                i = 2 * (m % 2) + k
                nc.scalar.copy(out=natural(o_sb[seg][m // 2][:, 512 * i : 512 * i + 512]), in_=even_odd(banks[k][:]))
                if tile_by_tile:
                    store(seg, m, k, 1)
            if not tile_by_tile:
                store(seg, m, 0, 2)

        def x1t_out(engine, n, banks):
            s, m = n // 4, n % 4
            for k in range(2):
                j = 2 * m + k
                copy_out(
                    engine,
                    y_grp[s][:, 512 * j : 512 * j + 512].rearrange("p (r t) -> p r t", t=4),
                    banks[k][:].rearrange("p (t r) -> p r t", t=4),
                )

        def quantise_x1t(n):
            s = n // 4
            quantise(y_grp[s], y_codes[s], y_scales[s], 256 * (n % 4))

        def x2_out(n, banks, tile_by_tile=False):
            seg, m = 2 * (n // 4) + 1, n % 4
            for k in range(2):
                i = 2 * (m % 2) + k
                j = 2 * m + k
                nc.vector.scalar_tensor_tensor(
                    out=natural(o_sb[seg][m // 2][:, 512 * i : 512 * i + 512]),
                    in0=even_odd(banks[k][:]),
                    scalar=2.0,
                    in1=natural(x_sb[:, 512 * j : 512 * j + 512]),
                    op0=MULT,
                    op1=SUBTRACT,
                )
                if tile_by_tile:
                    store(seg, m, k, 1)
            if not tile_by_tile:
                store(seg, m, 0, 2)

        a_banks = [transpose_pair(a_sb[0], [e, 2 + e]) for e in range(2)]
        x_banks = [transpose_pair(x_sb, [2 * m, 2 * m + 1]) for m in range(4)]
        regroup(nc.vector, a_banks[0], a_grp[0], 0)
        regroup(nc.scalar, a_banks[1], a_grp[0], 256)
        for e in range(2):
            quantise(a_grp[0], a_codes[0], a_scales[0], 256 * e)
        for m in range(3):
            regroup(nc.scalar, x_banks[m], x_grp, 256 * m)
            quantise(x_grp, x_codes, x_scales, 256 * m)

        t_banks = []

        def vector_copy(step):
            if step == 0:
                regroup(nc.vector, x_banks[3], x_grp, 768)
            elif step < 3:
                x1t_out(nc.vector, step - 1, t_banks[step - 1])
            else:
                regroup(nc.vector, a_banks[step - 3], a_grp[1], 256 * (step - 3))

        def vector_quantise(step):
            if step == 0:
                quantise(x_grp, x_codes, x_scales, 768)
            elif step < 3:
                quantise_x1t(step - 1)
            else:
                quantise(a_grp[1], a_codes[1], a_scales[1], 256 * (step - 3))

        for n in range(4):
            b1 = x1_passes(n)
            if n < 2:
                t_banks.append(x1t_passes(n))
            if n == 2:
                a_banks = [transpose_pair(a_sb[1], [e, 2 + e]) for e in range(2)]
            x1_out(n, b1, tile_by_tile=True)
            vector_copy(n)
            if n > 0:
                vector_quantise(n - 1)
        vector_copy(4)
        vector_quantise(3)
        vector_quantise(4)

        for k in range(3):
            for h in range(2):
                bt = x1t_passes(2 + 2 * k + h)
                b2 = x2_passes(2 * k + h)
                x1t_out(nc.scalar, 2 + 2 * k + h, bt)
                x2_out(2 * k + h, b2, tile_by_tile=True)
                quantise_x1t(2 + 2 * k + h)
            b1 = x1_passes(4 + k)
            x1_out(4 + k, b1, tile_by_tile=True)
        b1 = x1_passes(7)
        b2 = [x2_passes(6), x2_passes(7)]
        x2_out(6, b2[0], tile_by_tile=True)
        x1_out(7, b1, tile_by_tile=True)
        x2_out(7, b2[1], tile_by_tile=True)
